import numpy as np
import ml_dtypes


def mxq(x, axis, fmt="e4m3"):
    dtype, down = {"e4m3": (ml_dtypes.float8_e4m3fn, 7), "e5m2": (ml_dtypes.float8_e5m2, 14)}[fmt]
    v = np.moveaxis(np.asarray(x, np.float32).astype(ml_dtypes.bfloat16).astype(np.float64), axis, -1)
    blocks = v.reshape(v.shape[:-1] + (-1, 32))
    amax = np.abs(blocks).max(-1, keepdims=True)
    byte = np.maximum(np.where(amax > 0, np.frexp(amax)[1] - 1 + 127, 0) - down, 1)
    scale = np.exp2(byte - 127.0)
    codes = (blocks / scale).astype(np.float32).astype(dtype).astype(np.float64)
    return np.moveaxis((codes * scale).reshape(v.shape), -1, axis)


WIDE = False


def mx_kscale(k):
    if not WIDE:
        return np.ones(k)
    levels = np.array([10, -10, 5, -5, 0])
    a = np.random.permutation(np.resize(levels, k // 512 * 4)).reshape(k // 512, 4)
    idx = np.arange(k)
    return np.exp2(a[idx // 512, idx % 128 // 32])


BF16 = ml_dtypes.bfloat16


def bf(x):
    return np.asarray(x, np.float32).astype(BF16)


def f64(x):
    return np.asarray(x).astype(np.float64)


B, C, HH, WW, HD = 4, 512, 32, 32, 64
S = HH * WW
NH = C // HD
EPS = 1e-4


def mp_weight(w):
    o, i, kh, kw = w.shape
    fan_in = i * kh * kw
    n = np.sqrt(np.sum(w * w, axis=(1, 2, 3), keepdims=True))
    alpha = 1.0 / np.sqrt(fan_in)
    wn = w / (EPS + alpha * n) / np.sqrt(fan_in)
    return wn[:, :, 0, 0]


def pixel_norm(t):
    return t * (1.0 / np.sqrt(np.mean(t * t, axis=1, keepdims=True) + EPS))


def to_heads(t):
    return t.reshape(B, S, NH, HD).transpose(0, 2, 1, 3)


def setup_inputs():
    s = mx_kscale(C)
    sc = s * np.sqrt(np.mean(1.0 / s**2))
    gain = 0.002 * np.exp2(np.random.uniform(-2.0, 2.0, 3 * C))
    return {"x": bf(np.random.standard_normal((B, C, HH, WW)) * 0.06 * sc[None, :, None, None]),
            "w_attn": bf(np.random.standard_normal((3 * C, C, 1, 1)) * gain[:, None, None, None] / sc[None, :, None, None])}


def reference(x, w_attn):
    wn = mp_weight(f64(w_attn))
    xt = f64(x).reshape(B, C, S).transpose(0, 2, 1)
    p = mxq(xt, 2, "e4m3") @ mxq(wn.T, 0, "e4m3")
    q, k, v = np.split(p, 3, axis=-1)
    return pixel_norm(to_heads(q)), pixel_norm(to_heads(k)), pixel_norm(to_heads(v))

@@ -1,0 +1,239 @@
+import math
+from contextlib import ExitStack
+
+import concourse.mybir as mybir
+from concourse.masks import make_identity
+
+BF16 = mybir.dt.bfloat16
+F32 = mybir.dt.float32
+U32 = mybir.dt.uint32
+U8 = mybir.dt.uint8
+FP8X4 = mybir.dt.float8_e4m3fn_x4
+ACT = mybir.ActivationFunctionType
+ALU = mybir.AluOpType
+
+P = 128
+PACK = 4
+BATCH = 4
+CHANNELS = P * PACK
+POSITIONS = 1024
+HEADS = 8
+HEAD_DIM = 64
+COLS = HEADS * HEAD_DIM
+KINDS = 3
+W_TILES = COLS // P
+RUN = POSITIONS // P
+EPS = 1e-4
+TINY = 2.0**-80
+VECTOR_BANKS = 2
+LAG = 2
+
+FLOPS = 2 * BATCH * POSITIONS * CHANNELS * KINDS * COLS
+
+
+def tile_cosineattention_pa_t_kernel(tc, x, w_attn, out_0, out_1, out_2):
+    nc = tc.nc
+    outs = (out_0, out_1, out_2)
+    w_view = w_attn.rearrange("(j c p) k a b -> j p c (k a b)", j=KINDS, c=W_TILES, p=P)
+
+    with ExitStack() as stack:
+        keep = stack.enter_context(tc.tile_pool(name="keep", bufs=1))
+        x_in = stack.enter_context(tc.tile_pool(name="x_in", bufs=BATCH))
+        x_stage = stack.enter_context(tc.tile_pool(name="x_stage", bufs=2))
+        w_stage = stack.enter_context(tc.tile_pool(name="w_stage", bufs=2))
+        sq_pool = stack.enter_context(tc.tile_pool(name="sq_pool", bufs=3))
+        norm_pool = stack.enter_context(tc.tile_pool(name="norm_pool", bufs=3))
+        res_pool = stack.enter_context(tc.tile_pool(name="res_pool", bufs=3))
+        sq_psum = stack.enter_context(tc.psum_pool(name="sq_psum", bufs=3))
+        mul_psum = stack.enter_context(tc.psum_pool(name="mul_psum", bufs=3))
+        wt_psum = stack.enter_context(tc.psum_pool(name="wt_psum", bufs=2))
+
+        ident = keep.tile([P, P], BF16)
+        make_identity(nc, ident[:])
+        eps_col = keep.tile([P, 1], F32)
+        nc.vector.memset(eps_col[:], 0.0)
+        nc.vector.tensor_scalar_add(out=eps_col[:], in0=eps_col[:], scalar1=EPS)
+        tiny_col = keep.tile([P, 1], F32)
+        nc.vector.memset(tiny_col[:], TINY)
+        warm_col = keep.tile([P, 1], F32)
+        nc.scalar.activation(out=warm_col[:], in_=tiny_col[:], func=ACT.Abs_reciprocal_sqrt)
+
+        w_raw = keep.tile([P, KINDS, W_TILES, CHANNELS], BF16)
+        w_squares = keep.tile([P, KINDS, W_TILES, CHANNELS], BF16)
+        w_sumsq = keep.tile([P, KINDS, W_TILES], F32)
+        w_rsqrt = keep.tile([P, KINDS, W_TILES], F32)
+        w_norm = keep.tile([P, KINDS, W_TILES], F32)
+        w_denom = keep.tile([P, KINDS, W_TILES], F32)
+        w_inv = keep.tile([P, KINDS, W_TILES], F32)
+        w_codes = keep.tile([P, KINDS, COLS], U32, align_bytes=64)
+        w_scales = keep.tile([P, KINDS, COLS], U8, align_bytes=64)
+        x_codes = keep.tile([P, BATCH, POSITIONS], U32, align_bytes=64)
+        x_scales = keep.tile([P, BATCH, POSITIONS], U8, align_bytes=64)
+
+        x_raw = {}
+
+        def load_w(j):
+            nc.sync.dma_start(out=w_raw[:, j], in_=w_view[j])
+
+        def load_x(b):
+            raw = x_in.tile([P, PACK, POSITIONS], BF16)
+            nc.sync.dma_start(out=raw[:], in_=x[b].rearrange("(t p) h w -> p t (h w)", p=P))
+            x_raw[b] = raw
+
+        load_w(0)
+        load_x(0)
+        load_w(1)
+        load_w(2)
+        for b in range(1, BATCH):
+            load_x(b)
+
+        def filter_norms(j):
+            for c in range(W_TILES):
+                nc.scalar.activation(
+                    out=w_squares[:, j, c, :],
+                    in_=w_raw[:, j, c, :],
+                    func=ACT.Square,
+                    accum_out=w_sumsq[:, j, c : c + 1],
+                )
+            nc.scalar.activation(
+                out=w_rsqrt[:, j, :],
+                in_=w_sumsq[:, j, :],
+                func=ACT.Abs_reciprocal_sqrt,
+                bias=tiny_col[:],
+            )
+
+        def quantise_w(j):
+            nc.vector.tensor_tensor(
+                out=w_norm[:, j, :], in0=w_sumsq[:, j, :], in1=w_rsqrt[:, j, :], op=ALU.mult
+            )
+            nc.vector.tensor_scalar_add(
+                out=w_denom[:, j, :], in0=w_norm[:, j, :], scalar1=EPS * math.sqrt(CHANNELS)
+            )
+            nc.vector.reciprocal(out=w_inv[:, j, :], in_=w_denom[:, j, :])
+            wn = w_stage.tile([P, W_TILES, CHANNELS], BF16)
+            for c in range(W_TILES):
+                nc.vector.tensor_scalar_mul(
+                    out=wn[:, c, :], in0=w_raw[:, j, c, :], scalar1=w_inv[:, j, c : c + 1]
+                )
+            w_grouped = w_stage.tile([P, COLS, PACK], BF16, align_bytes=64)
+            for half in range(W_TILES // 2):
+                wt = wt_psum.tile([P, 2, PACK, P], BF16)
+                for c in range(2):
+                    for t in range(PACK):
+                        nc.tensor.transpose(
+                            wt[:, c, t, :], wn[:, 2 * half + c, t * P : (t + 1) * P], ident[:]
+                        )
+                nc.scalar.copy(
+                    out=w_grouped[:, 2 * P * half : 2 * P * (half + 1), :].rearrange(
+                        "p (c o) t -> p c o t", c=2
+                    ),
+                    in_=wt[:].rearrange("p c t o -> p c o t"),
+                )
+            nc.vector.quantize_mx(
+                out=w_codes[:, j, :].bitcast(FP8X4),
+                scales=w_scales[:, j, :],
+                in_=w_grouped[:].rearrange("p o t -> p (o t)"),
+            )
+
+        def quantise_x(b):
+            x_grouped = x_stage.tile([P, RUN, P, PACK], BF16, align_bytes=64)
+            source = x_raw[b][:].rearrange("p t (q r) -> p q t r", r=RUN)
+            for half in range(2):
+                rs = slice(half * RUN // 2, (half + 1) * RUN // 2)
+                nc.vector.tensor_copy(
+                    out=x_grouped[:, rs].rearrange("p r q t -> p q t r"), in_=source[:, :, :, rs]
+                )
+            nc.vector.quantize_mx(
+                out=x_codes[:, b, :].bitcast(FP8X4),
+                scales=x_scales[:, b, :],
+                in_=x_grouped[:].rearrange("p r q t -> p (r q t)"),
+            )
+
+        def project(pool, j, b, r):
+            bank = pool.tile([P, COLS], F32)
+            cols = slice(r * P, (r + 1) * P)
+            nc.tensor.matmul_mx(
+                out=bank[:],
+                lhsT=x_codes[:, b, cols].bitcast(FP8X4),
+                lhsT_scale=x_scales[:, b, cols],
+                rhs=w_codes[:, j, :].bitcast(FP8X4),
+                rhs_scale=w_scales[:, j, :],
+                start=True,
+                stop=True,
+            )
+            return bank
+
+        filter_norms(0)
+        quantise_w(0)
+        quantise_x(0)
+
+        units = [(j, b) for j in range(KINDS) for b in range(BATCH)]
+        squares_of = {}
+        sums_of = {}
+        rnorm_of = {}
+        for i in range(len(units) + LAG):
+            if i + 1 < BATCH:
+                quantise_x(i + 1)
+            if i < len(units):
+                squares = sq_pool.tile([P, RUN, HEADS, HEAD_DIM], F32)
+                squares_of[i] = squares
+            if i >= LAG:
+                result = res_pool.tile([P, HEADS, RUN, HEAD_DIM], F32)
+            for r in range(RUN):
+                if i < len(units):
+                    j, b = units[i]
+                    bank_sq = project(sq_psum, j, b, r)
+                    nc.scalar.activation(
+                        out=squares_of[i][:, r].rearrange("p n d -> p (n d)"),
+                        in_=bank_sq[:],
+                        func=ACT.Square,
+                    )
+                if i >= LAG:
+                    j, b = units[i - LAG]
+                    bank_mul = project(mul_psum, j, b, r)
+                    nc.vector.tensor_tensor(
+                        out=result[:, :, r, :],
+                        in0=bank_mul[:].rearrange("p (n d) -> p n d", n=HEADS),
+                        in1=rnorm_of[i - LAG][:, r, :].unsqueeze(1).to_broadcast([P, HEADS, HEAD_DIM]),
+                        op=ALU.mult,
+                    )
+            if i >= LAG:
+                j, b = units[i - LAG]
+                nc.sync.dma_start(
+                    out=outs[j][b].rearrange("n (q r) d -> q n (r d)", r=RUN),
+                    in_=result[:].rearrange("p n r d -> p n (r d)"),
+                )
+            if i < len(units):
+                sq = squares_of[i]
+                sums = norm_pool.tile([P, RUN, HEAD_DIM], F32)
+                sums_of[i] = sums
+                g = slice(0, RUN - VECTOR_BANKS)
+                v = slice(RUN - VECTOR_BANKS, RUN)
+                nc.vector.tensor_reduce(
+                    out=sums[:, v, :],
+                    in_=sq[:, v].rearrange("p r n d -> p r d n"),
+                    axis=mybir.AxisListType.X,
+                    op=ALU.add,
+                )
+                nc.gpsimd.tensor_tensor(
+                    out=sq[:, g, 0:4, :], in0=sq[:, g, 0:4, :], in1=sq[:, g, 4:8, :], op=ALU.add
+                )
+                nc.gpsimd.tensor_tensor(
+                    out=sq[:, g, 0:2, :], in0=sq[:, g, 0:2, :], in1=sq[:, g, 2:4, :], op=ALU.add
+                )
+                nc.gpsimd.tensor_tensor(
+                    out=sums[:, g, :], in0=sq[:, g, 0, :], in1=sq[:, g, 1, :], op=ALU.add
+                )
+            if i + 1 < KINDS:
+                filter_norms(i + 1)
+                quantise_w(i + 1)
+            if 1 <= i <= len(units):
+                rnorm = norm_pool.tile([P, RUN, HEAD_DIM], F32)
+                rnorm_of[i - 1] = rnorm
+                nc.scalar.activation(
+                    out=rnorm[:].rearrange("p r d -> p (r d)"),
+                    in_=sums_of[i - 1][:].rearrange("p r d -> p (r d)"),
+                    func=ACT.Abs_reciprocal_sqrt,
+                    scale=1.0 / HEADS,
+                    bias=eps_col[:],
+                )

@@ -25,7 +25,7 @@ W_TILES = COLS // P
 RUN = POSITIONS // P
 EPS = 1e-4
 TINY = 2.0**-80
-VECTOR_BANKS = 2
+VECTOR_BANKS = 3
 LAG = 2
 
 FLOPS = 2 * BATCH * POSITIONS * CHANNELS * KINDS * COLS

@@ -25,7 +25,9 @@ W_TILES = COLS // P
 RUN = POSITIONS // P
 EPS = 1e-4
 TINY = 2.0**-80
-VECTOR_BANKS = 3
+VECTOR_BANKS = 2
+GPSIMD_BANKS = RUN - VECTOR_BANKS
+HALF = RUN // 2
 LAG = 2
 
 FLOPS = 2 * BATCH * POSITIONS * CHANNELS * KINDS * COLS
@@ -112,8 +114,8 @@ def tile_cosineattention_pa_t_kernel(tc, x, w_attn, out_0, out_1, out_2):
             nc.vector.reciprocal(out=w_inv[:, j, :], in_=w_denom[:, j, :])
             wn = w_stage.tile([P, W_TILES, CHANNELS], BF16)
             for c in range(W_TILES):
-                nc.vector.tensor_scalar_mul(
-                    out=wn[:, c, :], in0=w_raw[:, j, c, :], scalar1=w_inv[:, j, c : c + 1]
+                nc.scalar.activation(
+                    out=wn[:, c, :], in_=w_raw[:, j, c, :], func=ACT.Copy, scale=w_inv[:, j, c : c + 1]
                 )
             w_grouped = w_stage.tile([P, COLS, PACK], BF16, align_bytes=64)
             for half in range(W_TILES // 2):
@@ -168,26 +170,32 @@ def tile_cosineattention_pa_t_kernel(tc, x, w_attn, out_0, out_1, out_2):
         quantise_x(0)
 
         units = [(j, b) for j in range(KINDS) for b in range(BATCH)]
-        squares_of = {}
         sums_of = {}
         rnorm_of = {}
         for i in range(len(units) + LAG):
             if i + 1 < BATCH:
                 quantise_x(i + 1)
             if i < len(units):
-                squares = sq_pool.tile([P, RUN, HEADS, HEAD_DIM], F32)
-                squares_of[i] = squares
+                sq_g = sq_pool.tile([P, GPSIMD_BANKS, HEADS, HEAD_DIM], F32)
+                sq_v = sq_pool.tile([P, VECTOR_BANKS, HEAD_DIM, HEADS], F32)
             if i >= LAG:
                 result = res_pool.tile([P, HEADS, RUN, HEAD_DIM], F32)
             for r in range(RUN):
                 if i < len(units):
                     j, b = units[i]
                     bank_sq = project(sq_psum, j, b, r)
-                    nc.scalar.activation(
-                        out=squares_of[i][:, r].rearrange("p n d -> p (n d)"),
-                        in_=bank_sq[:],
-                        func=ACT.Square,
-                    )
+                    if r < GPSIMD_BANKS:
+                        nc.scalar.activation(
+                            out=sq_g[:, r].rearrange("p n d -> p (n d)"),
+                            in_=bank_sq[:],
+                            func=ACT.Square,
+                        )
+                    else:
+                        nc.scalar.activation(
+                            out=sq_v[:, r - GPSIMD_BANKS],
+                            in_=bank_sq[:].rearrange("p (n d) -> p d n", n=HEADS),
+                            func=ACT.Square,
+                        )
                 if i >= LAG:
                     j, b = units[i - LAG]
                     bank_mul = project(mul_psum, j, b, r)
@@ -197,32 +205,32 @@ def tile_cosineattention_pa_t_kernel(tc, x, w_attn, out_0, out_1, out_2):
                         in1=rnorm_of[i - LAG][:, r, :].unsqueeze(1).to_broadcast([P, HEADS, HEAD_DIM]),
                         op=ALU.mult,
                     )
-            if i >= LAG:
-                j, b = units[i - LAG]
-                nc.sync.dma_start(
-                    out=outs[j][b].rearrange("n (q r) d -> q n (r d)", r=RUN),
-                    in_=result[:].rearrange("p n r d -> p n (r d)"),
-                )
+                    if r % HALF == HALF - 1:
+                        rs = slice(r + 1 - HALF, r + 1)
+                        nc.sync.dma_start(
+                            out=outs[j][b].rearrange("n (q r) d -> q n r d", r=RUN)[:, :, rs, :],
+                            in_=result[:, :, rs, :],
+                        )
             if i < len(units):
-                sq = squares_of[i]
                 sums = norm_pool.tile([P, RUN, HEAD_DIM], F32)
                 sums_of[i] = sums
-                g = slice(0, RUN - VECTOR_BANKS)
-                v = slice(RUN - VECTOR_BANKS, RUN)
-                nc.vector.tensor_reduce(
-                    out=sums[:, v, :],
-                    in_=sq[:, v].rearrange("p r n d -> p r d n"),
-                    axis=mybir.AxisListType.X,
+                nc.gpsimd.tensor_tensor(
+                    out=sq_g[:, :, 0:4, :], in0=sq_g[:, :, 0:4, :], in1=sq_g[:, :, 4:8, :], op=ALU.add
+                )
+                nc.gpsimd.tensor_tensor(
+                    out=sq_g[:, :, 0:2, :], in0=sq_g[:, :, 0:2, :], in1=sq_g[:, :, 2:4, :], op=ALU.add
+                )
+                nc.gpsimd.tensor_tensor(
+                    out=sums[:, 0:GPSIMD_BANKS, :],
+                    in0=sq_g[:, :, 0, :],
+                    in1=sq_g[:, :, 1, :],
                     op=ALU.add,
                 )
-                nc.gpsimd.tensor_tensor(
-                    out=sq[:, g, 0:4, :], in0=sq[:, g, 0:4, :], in1=sq[:, g, 4:8, :], op=ALU.add
-                )
-                nc.gpsimd.tensor_tensor(
-                    out=sq[:, g, 0:2, :], in0=sq[:, g, 0:2, :], in1=sq[:, g, 2:4, :], op=ALU.add
-                )
-                nc.gpsimd.tensor_tensor(
-                    out=sums[:, g, :], in0=sq[:, g, 0, :], in1=sq[:, g, 1, :], op=ALU.add
+                nc.vector.tensor_reduce(
+                    out=sums[:, GPSIMD_BANKS:RUN, :],
+                    in_=sq_v[:],
+                    axis=mybir.AxisListType.X,
+                    op=ALU.add,
                 )
             if i + 1 < KINDS:
                 filter_norms(i + 1)

@@ -25,7 +25,7 @@ W_TILES = COLS // P
 RUN = POSITIONS // P
 EPS = 1e-4
 TINY = 2.0**-80
-VECTOR_BANKS = 2
+VECTOR_BANKS = 3
 GPSIMD_BANKS = RUN - VECTOR_BANKS
 HALF = RUN // 2
 LAG = 2

@@ -114,8 +114,8 @@ def tile_cosineattention_pa_t_kernel(tc, x, w_attn, out_0, out_1, out_2):
             nc.vector.reciprocal(out=w_inv[:, j, :], in_=w_denom[:, j, :])
             wn = w_stage.tile([P, W_TILES, CHANNELS], BF16)
             for c in range(W_TILES):
-                nc.scalar.activation(
-                    out=wn[:, c, :], in_=w_raw[:, j, c, :], func=ACT.Copy, scale=w_inv[:, j, c : c + 1]
+                nc.vector.tensor_scalar_mul(
+                    out=wn[:, c, :], in0=w_raw[:, j, c, :], scalar1=w_inv[:, j, c : c + 1]
                 )
             w_grouped = w_stage.tile([P, COLS, PACK], BF16, align_bytes=64)
             for half in range(W_TILES // 2):

@@ -23,12 +23,19 @@ COLS = HEADS * HEAD_DIM
 KINDS = 3
 W_TILES = COLS // P
 RUN = POSITIONS // P
+HALF = RUN // 2
 EPS = 1e-4
 TINY = 2.0**-80
-VECTOR_BANKS = 3
-GPSIMD_BANKS = RUN - VECTOR_BANKS
-HALF = RUN // 2
-LAG = 2
+FIRST_UNITS = 2
+TURNED = 3
+GROUPS = {3: (2, 1), RUN: (4, 4)}
+SUMS_A_BANK = 4
+TURN_AFTER = 3
+FOLD_AFTER = 5
+ROOT_AT = 15
+X_AT = ((0, 1, 2), (4, 6, 9), (12, 14, 16))
+W_AT = ((4, 10, 12, 26), (14, 18, 20, 27))
+LAG = 20
 
 FLOPS = 2 * BATCH * POSITIONS * CHANNELS * KINDS * COLS
 
@@ -39,19 +46,22 @@ def tile_cosineattention_pa_t_kernel(tc, x, w_attn, out_0, out_1, out_2):
     w_view = w_attn.rearrange("(j c p) k a b -> j p c (k a b)", j=KINDS, c=W_TILES, p=P)
 
     with ExitStack() as stack:
+        stack.enter_context(tc.manual_schedule())
         keep = stack.enter_context(tc.tile_pool(name="keep", bufs=1))
         x_in = stack.enter_context(tc.tile_pool(name="x_in", bufs=BATCH))
         x_stage = stack.enter_context(tc.tile_pool(name="x_stage", bufs=2))
         w_stage = stack.enter_context(tc.tile_pool(name="w_stage", bufs=2))
         sq_pool = stack.enter_context(tc.tile_pool(name="sq_pool", bufs=3))
-        norm_pool = stack.enter_context(tc.tile_pool(name="norm_pool", bufs=3))
+        norm_pool = stack.enter_context(tc.tile_pool(name="norm_pool", bufs=4))
         res_pool = stack.enter_context(tc.tile_pool(name="res_pool", bufs=3))
         sq_psum = stack.enter_context(tc.psum_pool(name="sq_psum", bufs=3))
-        mul_psum = stack.enter_context(tc.psum_pool(name="mul_psum", bufs=3))
-        wt_psum = stack.enter_context(tc.psum_pool(name="wt_psum", bufs=2))
+        mul_psum = stack.enter_context(tc.psum_pool(name="mul_psum", bufs=4))
+        turn_psum = stack.enter_context(tc.psum_pool(name="turn_psum", bufs=1))
 
         ident = keep.tile([P, P], BF16)
         make_identity(nc, ident[:])
+        ident_f32 = keep.tile([P, P], F32)
+        make_identity(nc, ident_f32[:])
         eps_col = keep.tile([P, 1], F32)
         nc.vector.memset(eps_col[:], 0.0)
         nc.vector.tensor_scalar_add(out=eps_col[:], in0=eps_col[:], scalar1=EPS)
@@ -61,10 +71,10 @@ def tile_cosineattention_pa_t_kernel(tc, x, w_attn, out_0, out_1, out_2):
         nc.scalar.activation(out=warm_col[:], in_=tiny_col[:], func=ACT.Abs_reciprocal_sqrt)
 
         w_raw = keep.tile([P, KINDS, W_TILES, CHANNELS], BF16)
-        w_squares = keep.tile([P, KINDS, W_TILES, CHANNELS], BF16)
+        w_squares = keep.tile([P, W_TILES, CHANNELS], BF16)
         w_sumsq = keep.tile([P, KINDS, W_TILES], F32)
         w_rsqrt = keep.tile([P, KINDS, W_TILES], F32)
-        w_norm = keep.tile([P, KINDS, W_TILES], F32)
+        w_products = keep.tile([P, W_TILES, CHANNELS], BF16)
         w_denom = keep.tile([P, KINDS, W_TILES], F32)
         w_inv = keep.tile([P, KINDS, W_TILES], F32)
         w_codes = keep.tile([P, KINDS, COLS], U32, align_bytes=64)
@@ -74,29 +84,32 @@ def tile_cosineattention_pa_t_kernel(tc, x, w_attn, out_0, out_1, out_2):
 
         x_raw = {}
 
-        def load_w(j):
-            nc.sync.dma_start(out=w_raw[:, j], in_=w_view[j])
+        def load_w(j, tiles):
+            nc.sync.dma_start(out=w_raw[:, j, tiles], in_=w_view[j][:, tiles])
 
         def load_x(b):
             raw = x_in.tile([P, PACK, POSITIONS], BF16)
             nc.sync.dma_start(out=raw[:], in_=x[b].rearrange("(t p) h w -> p t (h w)", p=P))
             x_raw[b] = raw
 
-        load_w(0)
+        load_w(0, slice(0, 2))
+        load_w(0, slice(2, 4))
         load_x(0)
-        load_w(1)
-        load_w(2)
-        for b in range(1, BATCH):
-            load_x(b)
+        load_w(1, slice(0, 4))
+        load_x(1)
+        load_w(2, slice(0, 4))
+        load_x(2)
+        load_x(3)
 
-        def filter_norms(j):
-            for c in range(W_TILES):
-                nc.scalar.activation(
-                    out=w_squares[:, j, c, :],
-                    in_=w_raw[:, j, c, :],
-                    func=ACT.Square,
-                    accum_out=w_sumsq[:, j, c : c + 1],
-                )
+        def filter_norm(j, c):
+            nc.scalar.activation(
+                out=w_squares[:, c],
+                in_=w_raw[:, j, c, :],
+                func=ACT.Square,
+                accum_out=w_sumsq[:, j, c : c + 1],
+            )
+
+        def filter_root(j):
             nc.scalar.activation(
                 out=w_rsqrt[:, j, :],
                 in_=w_sumsq[:, j, :],
@@ -104,144 +117,283 @@ def tile_cosineattention_pa_t_kernel(tc, x, w_attn, out_0, out_1, out_2):
                 bias=tiny_col[:],
             )
 
-        def quantise_w(j):
-            nc.vector.tensor_tensor(
-                out=w_norm[:, j, :], in0=w_sumsq[:, j, :], in1=w_rsqrt[:, j, :], op=ALU.mult
+        def filter_norm_vector(j, c):
+            nc.vector.scalar_tensor_tensor(
+                out=w_products[:, c],
+                in0=w_raw[:, j, c, :],
+                scalar=1.0,
+                in1=w_raw[:, j, c, :],
+                op0=ALU.mult,
+                op1=ALU.mult,
+                accum_out=w_sumsq[:, j, c : c + 1],
             )
-            nc.vector.tensor_scalar_add(
-                out=w_denom[:, j, :], in0=w_norm[:, j, :], scalar1=EPS * math.sqrt(CHANNELS)
+
+        wn_of = {}
+
+        def scale_w(j):
+            nc.vector.tensor_scalar(
+                out=w_denom[:, j, :],
+                in0=w_rsqrt[:, j, :],
+                scalar1=EPS * math.sqrt(CHANNELS),
+                scalar2=1.0,
+                op0=ALU.mult,
+                op1=ALU.add,
             )
             nc.vector.reciprocal(out=w_inv[:, j, :], in_=w_denom[:, j, :])
             wn = w_stage.tile([P, W_TILES, CHANNELS], BF16)
+            wn_of[j] = wn
             for c in range(W_TILES):
-                nc.vector.tensor_scalar_mul(
-                    out=wn[:, c, :], in0=w_raw[:, j, c, :], scalar1=w_inv[:, j, c : c + 1]
+                nc.vector.tensor_scalar(
+                    out=wn[:, c, :],
+                    in0=w_raw[:, j, c, :],
+                    scalar1=w_rsqrt[:, j, c : c + 1],
+                    scalar2=w_inv[:, j, c : c + 1],
+                    op0=ALU.mult,
+                    op1=ALU.mult,
                 )
-            w_grouped = w_stage.tile([P, COLS, PACK], BF16, align_bytes=64)
+
+        turned_w_of = {}
+        w_grouped_of = {}
+
+        def turn_w(j):
             for half in range(W_TILES // 2):
-                wt = wt_psum.tile([P, 2, PACK, P], BF16)
+                wt = mul_psum.tile([P, 2, PACK, P], BF16, tag="bank")
+                turned_w_of[j, half] = wt
                 for c in range(2):
                     for t in range(PACK):
                         nc.tensor.transpose(
-                            wt[:, c, t, :], wn[:, 2 * half + c, t * P : (t + 1) * P], ident[:]
+                            wt[:, c, t, :], wn_of[j][:, 2 * half + c, t * P : (t + 1) * P], ident[:]
                         )
+
+        def group_w(j):
+            w_grouped = w_stage.tile([P, COLS, PACK], BF16, align_bytes=64)
+            w_grouped_of[j] = w_grouped
+            for half in range(W_TILES // 2):
                 nc.scalar.copy(
                     out=w_grouped[:, 2 * P * half : 2 * P * (half + 1), :].rearrange(
                         "p (c o) t -> p c o t", c=2
                     ),
-                    in_=wt[:].rearrange("p c t o -> p c o t"),
+                    in_=turned_w_of[j, half][:].rearrange("p c t o -> p c o t"),
                 )
+
+        def quantise_w(j):
             nc.vector.quantize_mx(
                 out=w_codes[:, j, :].bitcast(FP8X4),
                 scales=w_scales[:, j, :],
-                in_=w_grouped[:].rearrange("p o t -> p (o t)"),
+                in_=w_grouped_of[j][:].rearrange("p o t -> p (o t)"),
             )
 
-        def quantise_x(b):
-            x_grouped = x_stage.tile([P, RUN, P, PACK], BF16, align_bytes=64)
-            source = x_raw[b][:].rearrange("p t (q r) -> p q t r", r=RUN)
-            for half in range(2):
-                rs = slice(half * RUN // 2, (half + 1) * RUN // 2)
-                nc.vector.tensor_copy(
-                    out=x_grouped[:, rs].rearrange("p r q t -> p q t r"), in_=source[:, :, :, rs]
-                )
+        x_grouped_of = {}
+
+        def group_x(b, half):
+            if half == 0:
+                x_grouped = x_stage.tile([P, RUN, P, PACK], BF16, align_bytes=64)
+                x_grouped_of[b] = x_grouped
+            rs = slice(half * HALF, (half + 1) * HALF)
+            out = x_grouped_of[b][:, rs].rearrange("p r q t -> p q t r")
+            in_ = x_raw[b][:].rearrange("p t (q r) -> p q t r", r=RUN)[:, :, :, rs]
+            nc.vector.tensor_copy(out=out, in_=in_)
+
+        def quantise_x(b, half):
+            rs = slice(half * HALF, (half + 1) * HALF)
+            cols = slice(half * HALF * P, (half + 1) * HALF * P)
             nc.vector.quantize_mx(
-                out=x_codes[:, b, :].bitcast(FP8X4),
-                scales=x_scales[:, b, :],
-                in_=x_grouped[:].rearrange("p r q t -> p (r q t)"),
+                out=x_codes[:, b, cols].bitcast(FP8X4),
+                scales=x_scales[:, b, cols],
+                in_=x_grouped_of[b][:, rs].rearrange("p r q t -> p (r q t)"),
             )
 
-        def project(pool, j, b, r):
-            bank = pool.tile([P, COLS], F32)
-            cols = slice(r * P, (r + 1) * P)
+        def project(out, left, left_scale, right, right_scale):
             nc.tensor.matmul_mx(
-                out=bank[:],
-                lhsT=x_codes[:, b, cols].bitcast(FP8X4),
-                lhsT_scale=x_scales[:, b, cols],
-                rhs=w_codes[:, j, :].bitcast(FP8X4),
-                rhs_scale=w_scales[:, j, :],
+                out=out,
+                lhsT=left.bitcast(FP8X4),
+                lhsT_scale=left_scale,
+                rhs=right.bitcast(FP8X4),
+                rhs_scale=right_scale,
                 start=True,
                 stop=True,
             )
+
+        def project_positions(pool, j, b, r):
+            bank = pool.tile([P, COLS], F32, tag="bank")
+            cols = slice(r * P, (r + 1) * P)
+            project(bank[:], x_codes[:, b, cols], x_scales[:, b, cols], w_codes[:, j, :], w_scales[:, j, :])
             return bank
 
-        filter_norms(0)
-        quantise_w(0)
-        quantise_x(0)
-
         units = [(j, b) for j in range(KINDS) for b in range(BATCH)]
+        squares_of = {}
         sums_of = {}
+        turned_of = {}
         rnorm_of = {}
-        for i in range(len(units) + LAG):
-            if i + 1 < BATCH:
-                quantise_x(i + 1)
-            if i < len(units):
-                sq_g = sq_pool.tile([P, GPSIMD_BANKS, HEADS, HEAD_DIM], F32)
-                sq_v = sq_pool.tile([P, VECTOR_BANKS, HEAD_DIM, HEADS], F32)
-            if i >= LAG:
-                result = res_pool.tile([P, HEADS, RUN, HEAD_DIM], F32)
-            for r in range(RUN):
-                if i < len(units):
-                    j, b = units[i]
-                    bank_sq = project(sq_psum, j, b, r)
-                    if r < GPSIMD_BANKS:
-                        nc.scalar.activation(
-                            out=sq_g[:, r].rearrange("p n d -> p (n d)"),
-                            in_=bank_sq[:],
-                            func=ACT.Square,
-                        )
-                    else:
-                        nc.scalar.activation(
-                            out=sq_v[:, r - GPSIMD_BANKS],
-                            in_=bank_sq[:].rearrange("p (n d) -> p d n", n=HEADS),
-                            func=ACT.Square,
-                        )
-                if i >= LAG:
-                    j, b = units[i - LAG]
-                    bank_mul = project(mul_psum, j, b, r)
-                    nc.vector.tensor_tensor(
-                        out=result[:, :, r, :],
-                        in0=bank_mul[:].rearrange("p (n d) -> p n d", n=HEADS),
-                        in1=rnorm_of[i - LAG][:, r, :].unsqueeze(1).to_broadcast([P, HEADS, HEAD_DIM]),
-                        op=ALU.mult,
-                    )
-                    if r % HALF == HALF - 1:
-                        rs = slice(r + 1 - HALF, r + 1)
-                        nc.sync.dma_start(
-                            out=outs[j][b].rearrange("n (q r) d -> q n r d", r=RUN)[:, :, rs, :],
-                            in_=result[:, :, rs, :],
-                        )
-            if i < len(units):
+        result_of = {}
+
+        def turned_of_unit(i):
+            return RUN if i < FIRST_UNITS else TURNED
+
+        def turned_groups(t):
+            return [(sum(GROUPS[t][:k]), n) for k, n in enumerate(GROUPS[t])]
+
+        def square_bank(i, place):
+            j, b = units[i]
+            t = turned_of_unit(i)
+            if place == 0:
+                squares = sq_pool.tile([P, RUN, COLS], F32)
                 sums = norm_pool.tile([P, RUN, HEAD_DIM], F32)
+                squares_of[i] = squares
                 sums_of[i] = sums
+            if place < RUN - t:
+                bank = project_positions(sq_psum, j, b, place)
+            else:
+                m = place - (RUN - t)
+                first, n = [group for group in turned_groups(t) if group[0] <= m][-1]
+                tiles = W_TILES // n
+                bank = sq_psum.tile([P, COLS], F32, tag="bank")
+                cols = slice((RUN - t + first) * P, (RUN - t + first + n) * P)
+                for e in range(tiles):
+                    c = tiles * (m - first) + e
+                    filters = slice(c * P, (c + 1) * P)
+                    project(
+                        bank[:, e * n * P : (e + 1) * n * P],
+                        w_codes[:, j, filters],
+                        w_scales[:, j, filters],
+                        x_codes[:, b, cols],
+                        x_scales[:, b, cols],
+                    )
+            nc.scalar.activation(out=squares_of[i][:, place], in_=bank[:], func=ACT.Square)
+
+        def gpsimd_adds(i):
+            g = RUN - turned_of_unit(i)
+            squares = squares_of[i][:, 0:g].rearrange("p r (n d) -> p r n d", n=HEADS)
+            for heads in (4, 2):
                 nc.gpsimd.tensor_tensor(
-                    out=sq_g[:, :, 0:4, :], in0=sq_g[:, :, 0:4, :], in1=sq_g[:, :, 4:8, :], op=ALU.add
-                )
-                nc.gpsimd.tensor_tensor(
-                    out=sq_g[:, :, 0:2, :], in0=sq_g[:, :, 0:2, :], in1=sq_g[:, :, 2:4, :], op=ALU.add
-                )
-                nc.gpsimd.tensor_tensor(
-                    out=sums[:, 0:GPSIMD_BANKS, :],
-                    in0=sq_g[:, :, 0, :],
-                    in1=sq_g[:, :, 1, :],
+                    out=squares[:, :, 0:heads],
+                    in0=squares[:, :, 0:heads],
+                    in1=squares[:, :, heads : 2 * heads],
                     op=ALU.add,
                 )
-                nc.vector.tensor_reduce(
-                    out=sums[:, GPSIMD_BANKS:RUN, :],
-                    in_=sq_v[:],
-                    axis=mybir.AxisListType.X,
-                    op=ALU.add,
+            nc.gpsimd.tensor_tensor(
+                out=sums_of[i][:, 0:g], in0=squares[:, :, 0], in1=squares[:, :, 1], op=ALU.add
+            )
+
+        def sums_banks(t):
+            return [range(k, min(k + SUMS_A_BANK, t)) for k in range(0, t, SUMS_A_BANK)]
+
+        def turn_squares(i, part):
+            t = turned_of_unit(i)
+            positions = sums_banks(t)[part]
+            if i < FIRST_UNITS:
+                turned = mul_psum.tile([P, len(positions), P], F32, tag="bank")
+            else:
+                turned = turn_psum.tile([P, len(positions), P], F32, tag="turn")
+            turned_of[i, part] = turned
+            for first, n in turned_groups(t):
+                group = squares_of[i][:, RUN - t + first : RUN - t + first + n].rearrange(
+                    "p m (c q) -> p (m c) q", q=n * P
                 )
-            if i + 1 < KINDS:
-                filter_norms(i + 1)
-                quantise_w(i + 1)
-            if 1 <= i <= len(units):
-                rnorm = norm_pool.tile([P, RUN, HEAD_DIM], F32)
-                rnorm_of[i - 1] = rnorm
-                nc.scalar.activation(
-                    out=rnorm[:].rearrange("p r d -> p (r d)"),
-                    in_=sums_of[i - 1][:].rearrange("p r d -> p (r d)"),
-                    func=ACT.Abs_reciprocal_sqrt,
-                    scale=1.0 / HEADS,
-                    bias=eps_col[:],
+                for k in range(n):
+                    if first + k not in positions:
+                        continue
+                    for c in range(W_TILES):
+                        nc.tensor.matmul(
+                            turned[:, first + k - positions[0], :],
+                            lhsT=group[:, c, k * P : (k + 1) * P],
+                            rhs=ident_f32[:],
+                            is_transpose=True,
+                            start=c == 0,
+                            stop=c == W_TILES - 1,
+                        )
+
+        def fold(i, part):
+            t = turned_of_unit(i)
+            positions = sums_banks(t)[part]
+            nc.vector.tensor_reduce(
+                out=sums_of[i][:, RUN - t + positions[0] : RUN - t + positions[-1] + 1],
+                in_=turned_of[i, part][:].rearrange("p k (h d) -> p k d h", h=2),
+                axis=mybir.AxisListType.X,
+                op=ALU.add,
+            )
+
+        def inverse_root(i):
+            rnorm = norm_pool.tile([P, RUN, HEAD_DIM], F32)
+            rnorm_of[i] = rnorm
+            nc.scalar.activation(
+                out=rnorm[:].rearrange("p r d -> p (r d)"),
+                in_=sums_of[i][:].rearrange("p r d -> p (r d)"),
+                func=ACT.Abs_reciprocal_sqrt,
+                scale=1.0 / HEADS,
+                bias=eps_col[:],
+            )
+
+        def multiply_bank(i, r):
+            j, b = units[i]
+            if r == 0:
+                result = res_pool.tile([P, HEADS, RUN, HEAD_DIM], F32)
+                result_of[i] = result
+            bank = project_positions(mul_psum, j, b, r)
+            nc.vector.tensor_tensor(
+                out=result_of[i][:, :, r, :],
+                in0=bank[:].rearrange("p (n d) -> p n d", n=HEADS),
+                in1=rnorm_of[i][:, r, :].unsqueeze(1).to_broadcast([P, HEADS, HEAD_DIM]),
+                op=ALU.mult,
+            )
+            if r % HALF == HALF - 1:
+                rs = slice(r + 1 - HALF, r + 1)
+                nc.sync.dma_start(
+                    out=outs[j][b].rearrange("n (q r) d -> q n r d", r=RUN)[:, :, rs, :],
+                    in_=result_of[i][:, :, rs, :],
                 )
+
+        filter_norm(0, 0)
+        filter_norm_vector(0, 1)
+        filter_norm(0, 2)
+        filter_norm_vector(0, 3)
+        filter_root(0)
+        scale_w(0)
+        group_x(0, 0)
+        turn_w(0)
+        group_w(0)
+        for c in range(W_TILES):
+            filter_norm(1, c)
+        filter_root(1)
+        group_x(0, 1)
+        quantise_x(0, 0)
+        quantise_w(0)
+
+        steps = {}
+
+        def at(slot, *step):
+            steps.setdefault(slot, []).append(step)
+
+        at(0, quantise_x, 0, 1)
+        for b, (first, second, both) in enumerate(X_AT, start=1):
+            at(first, group_x, b, 0)
+            at(second, group_x, b, 1)
+            at(both, quantise_x, b, 0)
+            at(both, quantise_x, b, 1)
+        for c in range(W_TILES):
+            at(2 + 2 * c, filter_norm, 2, c)
+        at(8, filter_root, 2)
+        for j, (scale, turn, group, quantise) in enumerate(W_AT, start=1):
+            at(scale, scale_w, j)
+            at(turn, turn_w, j)
+            at(group, group_w, j)
+            at(quantise, quantise_w, j)
+        for i in range(len(units)):
+            t = turned_of_unit(i)
+            s = RUN * i
+            if t < RUN:
+                at(s + RUN - t - 1, gpsimd_adds, i)
+            for part, positions in enumerate(sums_banks(t)):
+                last = s + RUN - t + positions[-1]
+                at(last + TURN_AFTER, turn_squares, i, part)
+                at(last + FOLD_AFTER, fold, i, part)
+            at(s + ROOT_AT, inverse_root, i)
+
+        banks = RUN * len(units)
+        for slot in range(banks + LAG):
+            if slot < banks:
+                square_bank(slot // RUN, slot % RUN)
+            for action, *arguments in steps.get(slot, ()):
+                action(*arguments)
+            if slot >= LAG:
+                multiply_bank((slot - LAG) // RUN, (slot - LAG) % RUN)

@@ -26,16 +26,17 @@ RUN = POSITIONS // P
 HALF = RUN // 2
 EPS = 1e-4
 TINY = 2.0**-80
-FIRST_UNITS = 2
-TURNED = 3
-GROUPS = {3: (2, 1), RUN: (4, 4)}
+FIRST_SHARES = ((0, RUN), (0, RUN))
+SHARES = ((5, 2), (5, 2), (4, 3))
+GROUPS = {2: (2,), 3: (2, 1), RUN: (4, 4)}
 SUMS_A_BANK = 4
 TURN_AFTER = 3
-FOLD_AFTER = 5
-ROOT_AT = 15
-X_AT = ((0, 1, 2), (4, 6, 9), (12, 14, 16))
-W_AT = ((4, 10, 12, 26), (14, 18, 20, 27))
-LAG = 20
+FOLD_AFTER = 4
+REDUCE_AT = RUN + 1
+LAG = 2 * RUN + 1
+ROOT_AT = LAG - 1
+X_AT = ((0, 1, 2), (4, 5, 7), (8, 9, 11))
+W_AT = ((1, 1, 5, (16, 20), 24), (6, 2, 16, (37, 45), 54))
 
 FLOPS = 2 * BATCH * POSITIONS * CHANNELS * KINDS * COLS
 
@@ -155,32 +156,34 @@ def tile_cosineattention_pa_t_kernel(tc, x, w_attn, out_0, out_1, out_2):
         turned_w_of = {}
         w_grouped_of = {}
 
-        def turn_w(j):
-            for half in range(W_TILES // 2):
+        def turn_w(j, half):
+            if j == 0:
                 wt = mul_psum.tile([P, 2, PACK, P], BF16, tag="bank")
-                turned_w_of[j, half] = wt
-                for c in range(2):
-                    for t in range(PACK):
-                        nc.tensor.transpose(
-                            wt[:, c, t, :], wn_of[j][:, 2 * half + c, t * P : (t + 1) * P], ident[:]
-                        )
+            else:
+                wt = turn_psum.tile([P, 2, PACK, P], BF16, tag="turn")
+            turned_w_of[j, half] = wt
+            for c in range(2):
+                for t in range(PACK):
+                    nc.tensor.transpose(
+                        wt[:, c, t, :], wn_of[j][:, 2 * half + c, t * P : (t + 1) * P], ident[:]
+                    )
 
-        def group_w(j):
-            w_grouped = w_stage.tile([P, COLS, PACK], BF16, align_bytes=64)
-            w_grouped_of[j] = w_grouped
-            for half in range(W_TILES // 2):
-                nc.scalar.copy(
-                    out=w_grouped[:, 2 * P * half : 2 * P * (half + 1), :].rearrange(
-                        "p (c o) t -> p c o t", c=2
-                    ),
-                    in_=turned_w_of[j, half][:].rearrange("p c t o -> p c o t"),
-                )
+        def group_w(j, half):
+            if half == 0:
+                w_grouped = w_stage.tile([P, COLS, PACK], BF16, align_bytes=64)
+                w_grouped_of[j] = w_grouped
+            nc.scalar.copy(
+                out=w_grouped_of[j][:, 2 * P * half : 2 * P * (half + 1), :].rearrange(
+                    "p (c o) t -> p c o t", c=2
+                ),
+                in_=turned_w_of[j, half][:].rearrange("p c t o -> p c o t"),
+            )
 
-        def quantise_w(j):
+        def quantise_w(j, cols):
             nc.vector.quantize_mx(
-                out=w_codes[:, j, :].bitcast(FP8X4),
-                scales=w_scales[:, j, :],
-                in_=w_grouped_of[j][:].rearrange("p o t -> p (o t)"),
+                out=w_codes[:, j, cols].bitcast(FP8X4),
+                scales=w_scales[:, j, cols],
+                in_=w_grouped_of[j][:, cols].rearrange("p o t -> p (o t)"),
             )
 
         x_grouped_of = {}
@@ -227,30 +230,29 @@ def tile_cosineattention_pa_t_kernel(tc, x, w_attn, out_0, out_1, out_2):
         rnorm_of = {}
         result_of = {}
 
-        def turned_of_unit(i):
-            return RUN if i < FIRST_UNITS else TURNED
+        def shares(i):
+            g, t = FIRST_SHARES[i] if i < len(FIRST_SHARES) else SHARES[i % len(SHARES)]
+            return g, t, RUN - g - t
 
         def turned_groups(t):
             return [(sum(GROUPS[t][:k]), n) for k, n in enumerate(GROUPS[t])]
 
         def square_bank(i, place):
             j, b = units[i]
-            t = turned_of_unit(i)
+            g, t, v = shares(i)
             if place == 0:
                 squares = sq_pool.tile([P, RUN, COLS], F32)
                 sums = norm_pool.tile([P, RUN, HEAD_DIM], F32)
                 squares_of[i] = squares
                 sums_of[i] = sums
-            if place < RUN - t:
-                bank = project_positions(sq_psum, j, b, place)
-            else:
-                m = place - (RUN - t)
-                first, n = [group for group in turned_groups(t) if group[0] <= m][-1]
+            out = squares_of[i][:, place]
+            if g <= place < g + t:
+                first, n = [group for group in turned_groups(t) if group[0] <= place - g][-1]
                 tiles = W_TILES // n
                 bank = sq_psum.tile([P, COLS], F32, tag="bank")
-                cols = slice((RUN - t + first) * P, (RUN - t + first + n) * P)
+                cols = slice((g + first) * P, (g + first + n) * P)
                 for e in range(tiles):
-                    c = tiles * (m - first) + e
+                    c = tiles * (place - g - first) + e
                     filters = slice(c * P, (c + 1) * P)
                     project(
                         bank[:, e * n * P : (e + 1) * n * P],
@@ -259,10 +261,17 @@ def tile_cosineattention_pa_t_kernel(tc, x, w_attn, out_0, out_1, out_2):
                         x_codes[:, b, cols],
                         x_scales[:, b, cols],
                     )
-            nc.scalar.activation(out=squares_of[i][:, place], in_=bank[:], func=ACT.Square)
+                in_ = bank[:]
+            else:
+                bank = project_positions(sq_psum, j, b, place)
+                in_ = bank[:]
+                if place >= g + t:
+                    out = out.rearrange("p (d n) -> p d n", n=HEADS)
+                    in_ = in_.rearrange("p (n d) -> p d n", n=HEADS)
+            nc.scalar.activation(out=out, in_=in_, func=ACT.Square)
 
         def gpsimd_adds(i):
-            g = RUN - turned_of_unit(i)
+            g = shares(i)[0]
             squares = squares_of[i][:, 0:g].rearrange("p r (n d) -> p r n d", n=HEADS)
             for heads in (4, 2):
                 nc.gpsimd.tensor_tensor(
@@ -275,19 +284,28 @@ def tile_cosineattention_pa_t_kernel(tc, x, w_attn, out_0, out_1, out_2):
                 out=sums_of[i][:, 0:g], in0=squares[:, :, 0], in1=squares[:, :, 1], op=ALU.add
             )
 
+        def vector_adds(i):
+            g, t, v = shares(i)
+            nc.vector.tensor_reduce(
+                out=sums_of[i][:, g + t : RUN],
+                in_=squares_of[i][:, g + t : RUN].rearrange("p r (d n) -> p r d n", n=HEADS),
+                axis=mybir.AxisListType.X,
+                op=ALU.add,
+            )
+
         def sums_banks(t):
             return [range(k, min(k + SUMS_A_BANK, t)) for k in range(0, t, SUMS_A_BANK)]
 
         def turn_squares(i, part):
-            t = turned_of_unit(i)
+            g, t, v = shares(i)
             positions = sums_banks(t)[part]
-            if i < FIRST_UNITS:
+            if i < len(FIRST_SHARES):
                 turned = mul_psum.tile([P, len(positions), P], F32, tag="bank")
             else:
                 turned = turn_psum.tile([P, len(positions), P], F32, tag="turn")
             turned_of[i, part] = turned
             for first, n in turned_groups(t):
-                group = squares_of[i][:, RUN - t + first : RUN - t + first + n].rearrange(
+                group = squares_of[i][:, g + first : g + first + n].rearrange(
                     "p m (c q) -> p (m c) q", q=n * P
                 )
                 for k in range(n):
@@ -304,10 +322,10 @@ def tile_cosineattention_pa_t_kernel(tc, x, w_attn, out_0, out_1, out_2):
                         )
 
         def fold(i, part):
-            t = turned_of_unit(i)
+            g, t, v = shares(i)
             positions = sums_banks(t)[part]
             nc.vector.tensor_reduce(
-                out=sums_of[i][:, RUN - t + positions[0] : RUN - t + positions[-1] + 1],
+                out=sums_of[i][:, g + positions[0] : g + positions[-1] + 1],
                 in_=turned_of[i, part][:].rearrange("p k (h d) -> p k d h", h=2),
                 axis=mybir.AxisListType.X,
                 op=ALU.add,
@@ -350,14 +368,13 @@ def tile_cosineattention_pa_t_kernel(tc, x, w_attn, out_0, out_1, out_2):
         filter_root(0)
         scale_w(0)
         group_x(0, 0)
-        turn_w(0)
-        group_w(0)
-        for c in range(W_TILES):
-            filter_norm(1, c)
-        filter_root(1)
-        group_x(0, 1)
+        for half in range(2):
+            turn_w(0, half)
+            group_w(0, half)
         quantise_x(0, 0)
-        quantise_w(0)
+        quantise_w(0, slice(0, COLS // 2))
+        group_x(0, 1)
+        quantise_w(0, slice(COLS // 2, COLS))
 
         steps = {}
 
@@ -370,23 +387,26 @@ def tile_cosineattention_pa_t_kernel(tc, x, w_attn, out_0, out_1, out_2):
             at(second, group_x, b, 1)
             at(both, quantise_x, b, 0)
             at(both, quantise_x, b, 1)
-        for c in range(W_TILES):
-            at(2 + 2 * c, filter_norm, 2, c)
-        at(8, filter_root, 2)
-        for j, (scale, turn, group, quantise) in enumerate(W_AT, start=1):
+        for j, (norm, step, scale, turns, quantise) in enumerate(W_AT, start=1):
+            for c in range(W_TILES):
+                at(norm + step * c, filter_norm, j, c)
+            at(norm + step * (W_TILES - 1), filter_root, j)
             at(scale, scale_w, j)
-            at(turn, turn_w, j)
-            at(group, group_w, j)
-            at(quantise, quantise_w, j)
+            for half, slot in enumerate(turns):
+                at(slot, turn_w, j, half)
+                at(slot + 2, group_w, j, half)
+            at(quantise, quantise_w, j, slice(0, COLS))
         for i in range(len(units)):
-            t = turned_of_unit(i)
+            g, t, v = shares(i)
             s = RUN * i
-            if t < RUN:
-                at(s + RUN - t - 1, gpsimd_adds, i)
+            if g:
+                at(s + g - 1, gpsimd_adds, i)
             for part, positions in enumerate(sums_banks(t)):
-                last = s + RUN - t + positions[-1]
+                last = s + g + positions[-1]
                 at(last + TURN_AFTER, turn_squares, i, part)
                 at(last + FOLD_AFTER, fold, i, part)
+            if v:
+                at(s + REDUCE_AT, vector_adds, i)
             at(s + ROOT_AT, inverse_root, i)
 
         banks = RUN * len(units)

@@ -26,9 +26,9 @@ RUN = POSITIONS // P
 HALF = RUN // 2
 EPS = 1e-4
 TINY = 2.0**-80
-FIRST_SHARES = ((0, RUN), (0, RUN))
-SHARES = ((5, 2), (5, 2), (4, 3))
-GROUPS = {2: (2,), 3: (2, 1), RUN: (4, 4)}
+FIRST_SHARES = ((0, RUN), (0, 6))
+SHARES = (5, 2)
+GROUPS = {2: (2,), 6: (4, 2), RUN: (4, 4)}
 SUMS_A_BANK = 4
 TURN_AFTER = 3
 FOLD_AFTER = 4
@@ -36,7 +36,7 @@ REDUCE_AT = RUN + 1
 LAG = 2 * RUN + 1
 ROOT_AT = LAG - 1
 X_AT = ((0, 1, 2), (4, 5, 7), (8, 9, 11))
-W_AT = ((1, 1, 5, (16, 20), 24), (6, 2, 16, (37, 45), 54))
+W_AT = ((1, 1, 6, (16, 20), 26), (8, 2, 17, (36, 44), 60))
 
 FLOPS = 2 * BATCH * POSITIONS * CHANNELS * KINDS * COLS
 
@@ -131,7 +131,7 @@ def tile_cosineattention_pa_t_kernel(tc, x, w_attn, out_0, out_1, out_2):
 
         wn_of = {}
 
-        def scale_w(j):
+        def denominator_w(j):
             nc.vector.tensor_scalar(
                 out=w_denom[:, j, :],
                 in0=w_rsqrt[:, j, :],
@@ -140,7 +140,11 @@ def tile_cosineattention_pa_t_kernel(tc, x, w_attn, out_0, out_1, out_2):
                 op0=ALU.mult,
                 op1=ALU.add,
             )
+
+        def factor_w(j):
             nc.vector.reciprocal(out=w_inv[:, j, :], in_=w_denom[:, j, :])
+
+        def scale_w(j):
             wn = w_stage.tile([P, W_TILES, CHANNELS], BF16)
             wn_of[j] = wn
             for c in range(W_TILES):
@@ -231,7 +235,7 @@ def tile_cosineattention_pa_t_kernel(tc, x, w_attn, out_0, out_1, out_2):
         result_of = {}
 
         def shares(i):
-            g, t = FIRST_SHARES[i] if i < len(FIRST_SHARES) else SHARES[i % len(SHARES)]
+            g, t = FIRST_SHARES[i] if i < len(FIRST_SHARES) else SHARES
             return g, t, RUN - g - t
 
         def turned_groups(t):
@@ -366,6 +370,8 @@ def tile_cosineattention_pa_t_kernel(tc, x, w_attn, out_0, out_1, out_2):
         filter_norm(0, 2)
         filter_norm_vector(0, 3)
         filter_root(0)
+        denominator_w(0)
+        factor_w(0)
         scale_w(0)
         group_x(0, 0)
         for half in range(2):
@@ -391,6 +397,8 @@ def tile_cosineattention_pa_t_kernel(tc, x, w_attn, out_0, out_1, out_2):
             for c in range(W_TILES):
                 at(norm + step * c, filter_norm, j, c)
             at(norm + step * (W_TILES - 1), filter_root, j)
+            at(scale - 2, denominator_w, j)
+            at(scale - 1, factor_w, j)
             at(scale, scale_w, j)
             for half, slot in enumerate(turns):
                 at(slot, turn_w, j, half)

@@ -26,9 +26,10 @@ RUN = POSITIONS // P
 HALF = RUN // 2
 EPS = 1e-4
 TINY = 2.0**-80
-FIRST_SHARES = ((0, RUN), (0, 6))
+FIRST_SHARES = ((0, RUN), (0, 4))
 SHARES = (5, 2)
-GROUPS = {2: (2,), 6: (4, 2), RUN: (4, 4)}
+LAST_SHARES = (4, 3)
+GROUPS = {2: (2,), 3: (2, 1), 4: (4,), RUN: (4, 4)}
 SUMS_A_BANK = 4
 TURN_AFTER = 3
 FOLD_AFTER = 4
@@ -36,7 +37,7 @@ REDUCE_AT = RUN + 1
 LAG = 2 * RUN + 1
 ROOT_AT = LAG - 1
 X_AT = ((0, 1, 2), (4, 5, 7), (8, 9, 11))
-W_AT = ((1, 1, 6, (16, 20), 26), (8, 2, 17, (36, 44), 60))
+W_AT = ((1, 1, 8, (16, 20), 28), (8, 2, 17, (28, 44), 60))
 
 FLOPS = 2 * BATCH * POSITIONS * CHANNELS * KINDS * COLS
 
@@ -235,7 +236,10 @@ def tile_cosineattention_pa_t_kernel(tc, x, w_attn, out_0, out_1, out_2):
         result_of = {}
 
         def shares(i):
-            g, t = FIRST_SHARES[i] if i < len(FIRST_SHARES) else SHARES
+            if i < len(FIRST_SHARES):
+                g, t = FIRST_SHARES[i]
+            else:
+                g, t = LAST_SHARES if i == len(units) - 1 else SHARES
             return g, t, RUN - g - t
 
         def turned_groups(t):

@@ -350,23 +350,35 @@ def tile_cosineattention_pa_t_kernel(tc, x, w_attn, out_0, out_1, out_2):
                 bias=eps_col[:],
             )
 
-        def multiply_bank(i, r):
+        def multiply_bank(i, m):
             j, b = units[i]
-            if r == 0:
+            if m == 0:
                 result = res_pool.tile([P, HEADS, RUN, HEAD_DIM], F32)
                 result_of[i] = result
-            bank = project_positions(mul_psum, j, b, r)
+            side, pair = divmod(m, RUN // 2)
+            heads = slice(side * HEADS // 2, (side + 1) * HEADS // 2)
+            rs = slice(2 * pair, 2 * pair + 2)
+            filters = slice(side * COLS // 2, (side + 1) * COLS // 2)
+            bank = mul_psum.tile([P, COLS], F32, tag="bank")
+            for e in range(2):
+                cols = slice((2 * pair + e) * P, (2 * pair + e + 1) * P)
+                project(
+                    bank[:, e * COLS // 2 : (e + 1) * COLS // 2],
+                    x_codes[:, b, cols],
+                    x_scales[:, b, cols],
+                    w_codes[:, j, filters],
+                    w_scales[:, j, filters],
+                )
             nc.vector.tensor_tensor(
-                out=result_of[i][:, :, r, :],
-                in0=bank[:].rearrange("p (n d) -> p n d", n=HEADS),
-                in1=rnorm_of[i][:, r, :].unsqueeze(1).to_broadcast([P, HEADS, HEAD_DIM]),
+                out=result_of[i][:, heads, rs, :].rearrange("p n r d -> p r n d"),
+                in0=bank[:].rearrange("p (r n d) -> p r n d", r=2, n=HEADS // 2),
+                in1=rnorm_of[i][:, rs, :].unsqueeze(2).to_broadcast([P, 2, HEADS // 2, HEAD_DIM]),
                 op=ALU.mult,
             )
-            if r % HALF == HALF - 1:
-                rs = slice(r + 1 - HALF, r + 1)
+            if pair == RUN // 2 - 1:
                 nc.sync.dma_start(
-                    out=outs[j][b].rearrange("n (q r) d -> q n r d", r=RUN)[:, :, rs, :],
-                    in_=result_of[i][:, :, rs, :],
+                    out=outs[j][b].rearrange("n (q r) d -> q n r d", r=RUN)[:, heads],
+                    in_=result_of[i][:, heads],
                 )
 
         filter_norm(0, 0)

import math
from contextlib import ExitStack

import concourse.mybir as mybir
from concourse.masks import make_identity

BF16 = mybir.dt.bfloat16
F32 = mybir.dt.float32
U32 = mybir.dt.uint32
U8 = mybir.dt.uint8
FP8X4 = mybir.dt.float8_e4m3fn_x4
ACT = mybir.ActivationFunctionType
ALU = mybir.AluOpType

P = 128
PACK = 4
BATCH = 4
CHANNELS = P * PACK
POSITIONS = 1024
HEADS = 8
HEAD_DIM = 64
COLS = HEADS * HEAD_DIM
KINDS = 3
W_TILES = COLS // P
RUN = POSITIONS // P
HALF = RUN // 2
EPS = 1e-4
TINY = 2.0**-80
FIRST_SHARES = ((0, RUN), (0, 4))
SHARES = (5, 2)
LAST_SHARES = (4, 3)
GROUPS = {2: (2,), 3: (2, 1), 4: (4,), RUN: (4, 4)}
SUMS_A_BANK = 4
TURN_AFTER = 3
FOLD_AFTER = 4
REDUCE_AT = RUN + 1
LAG = 2 * RUN + 1
ROOT_AT = LAG - 1
X_AT = ((0, 1, 2), (4, 5, 7), (8, 9, 11))
W_AT = ((1, 1, 8, (16, 20), 28), (8, 2, 17, (28, 44), 60))

FLOPS = 2 * BATCH * POSITIONS * CHANNELS * KINDS * COLS


def tile_cosineattention_pa_t_kernel(tc, x, w_attn, out_0, out_1, out_2):
    nc = tc.nc
    outs = (out_0, out_1, out_2)
    w_view = w_attn.rearrange("(j c p) k a b -> j p c (k a b)", j=KINDS, c=W_TILES, p=P)

    with ExitStack() as stack:
        stack.enter_context(tc.manual_schedule())
        keep = stack.enter_context(tc.tile_pool(name="keep", bufs=1))
        x_in = stack.enter_context(tc.tile_pool(name="x_in", bufs=BATCH))
        x_stage = stack.enter_context(tc.tile_pool(name="x_stage", bufs=2))
        w_stage = stack.enter_context(tc.tile_pool(name="w_stage", bufs=2))
        sq_pool = stack.enter_context(tc.tile_pool(name="sq_pool", bufs=3))
        norm_pool = stack.enter_context(tc.tile_pool(name="norm_pool", bufs=4))
        res_pool = stack.enter_context(tc.tile_pool(name="res_pool", bufs=3))
        sq_psum = stack.enter_context(tc.psum_pool(name="sq_psum", bufs=3))
        mul_psum = stack.enter_context(tc.psum_pool(name="mul_psum", bufs=4))
        turn_psum = stack.enter_context(tc.psum_pool(name="turn_psum", bufs=1))

        ident = keep.tile([P, P], BF16)
        make_identity(nc, ident[:])
        ident_f32 = keep.tile([P, P], F32)
        make_identity(nc, ident_f32[:])
        eps_col = keep.tile([P, 1], F32)
        nc.vector.memset(eps_col[:], 0.0)
        nc.vector.tensor_scalar_add(out=eps_col[:], in0=eps_col[:], scalar1=EPS)
        tiny_col = keep.tile([P, 1], F32)
        nc.vector.memset(tiny_col[:], TINY)
        warm_col = keep.tile([P, 1], F32)
        nc.scalar.activation(out=warm_col[:], in_=tiny_col[:], func=ACT.Abs_reciprocal_sqrt)

        w_raw = keep.tile([P, KINDS, W_TILES, CHANNELS], BF16)
        w_squares = keep.tile([P, W_TILES, CHANNELS], BF16)
        w_sumsq = keep.tile([P, KINDS, W_TILES], F32)
        w_rsqrt = keep.tile([P, KINDS, W_TILES], F32)
        w_products = keep.tile([P, W_TILES, CHANNELS], BF16)
        w_denom = keep.tile([P, KINDS, W_TILES], F32)
        w_inv = keep.tile([P, KINDS, W_TILES], F32)
        w_codes = keep.tile([P, KINDS, COLS], U32, align_bytes=64)
        w_scales = keep.tile([P, KINDS, COLS], U8, align_bytes=64)
        x_codes = keep.tile([P, BATCH, POSITIONS], U32, align_bytes=64)
        x_scales = keep.tile([P, BATCH, POSITIONS], U8, align_bytes=64)

        x_raw = {}

        def load_w(j, tiles):
            nc.sync.dma_start(out=w_raw[:, j, tiles], in_=w_view[j][:, tiles])

        def load_x(b):
            raw = x_in.tile([P, PACK, POSITIONS], BF16)
            nc.sync.dma_start(out=raw[:], in_=x[b].rearrange("(t p) h w -> p t (h w)", p=P))
            x_raw[b] = raw

        load_w(0, slice(0, 2))
        load_w(0, slice(2, 4))
        load_x(0)
        load_w(1, slice(0, 4))
        load_x(1)
        load_w(2, slice(0, 4))
        load_x(2)
        load_x(3)

        def filter_norm(j, c):
            nc.scalar.activation(
                out=w_squares[:, c],
                in_=w_raw[:, j, c, :],
                func=ACT.Square,
                accum_out=w_sumsq[:, j, c : c + 1],
            )

        def filter_root(j):
            nc.scalar.activation(
                out=w_rsqrt[:, j, :],
                in_=w_sumsq[:, j, :],
                func=ACT.Abs_reciprocal_sqrt,
                bias=tiny_col[:],
            )

        def filter_norm_vector(j, c):
            nc.vector.scalar_tensor_tensor(
                out=w_products[:, c],
                in0=w_raw[:, j, c, :],
                scalar=1.0,
                in1=w_raw[:, j, c, :],
                op0=ALU.mult,
                op1=ALU.mult,
                accum_out=w_sumsq[:, j, c : c + 1],
            )

        wn_of = {}

        def denominator_w(j):
            nc.vector.tensor_scalar(
                out=w_denom[:, j, :],
                in0=w_rsqrt[:, j, :],
                scalar1=EPS * math.sqrt(CHANNELS),
                scalar2=1.0,
                op0=ALU.mult,
                op1=ALU.add,
            )

        def factor_w(j):
            nc.vector.reciprocal(out=w_inv[:, j, :], in_=w_denom[:, j, :])

        def scale_w(j):
            wn = w_stage.tile([P, W_TILES, CHANNELS], BF16)
            wn_of[j] = wn
            for c in range(W_TILES):
                nc.vector.tensor_scalar(
                    out=wn[:, c, :],
                    in0=w_raw[:, j, c, :],
                    scalar1=w_rsqrt[:, j, c : c + 1],
                    scalar2=w_inv[:, j, c : c + 1],
                    op0=ALU.mult,
                    op1=ALU.mult,
                )

        turned_w_of = {}
        w_grouped_of = {}

        def turn_w(j, half):
            if j == 0:
                wt = mul_psum.tile([P, 2, PACK, P], BF16, tag="bank")
            else:
                wt = turn_psum.tile([P, 2, PACK, P], BF16, tag="turn")
            turned_w_of[j, half] = wt
            for c in range(2):
                for t in range(PACK):
                    nc.tensor.transpose(
                        wt[:, c, t, :], wn_of[j][:, 2 * half + c, t * P : (t + 1) * P], ident[:]
                    )

        def group_w(j, half):
            if half == 0:
                w_grouped = w_stage.tile([P, COLS, PACK], BF16, align_bytes=64)
                w_grouped_of[j] = w_grouped
            nc.scalar.copy(
                out=w_grouped_of[j][:, 2 * P * half : 2 * P * (half + 1), :].rearrange(
                    "p (c o) t -> p c o t", c=2
                ),
                in_=turned_w_of[j, half][:].rearrange("p c t o -> p c o t"),
            )

        def quantise_w(j, cols):
            nc.vector.quantize_mx(
                out=w_codes[:, j, cols].bitcast(FP8X4),
                scales=w_scales[:, j, cols],
                in_=w_grouped_of[j][:, cols].rearrange("p o t -> p (o t)"),
            )

        x_grouped_of = {}

        def group_x(b, half):
            if half == 0:
                x_grouped = x_stage.tile([P, RUN, P, PACK], BF16, align_bytes=64)
                x_grouped_of[b] = x_grouped
            rs = slice(half * HALF, (half + 1) * HALF)
            out = x_grouped_of[b][:, rs].rearrange("p r q t -> p q t r")
            in_ = x_raw[b][:].rearrange("p t (q r) -> p q t r", r=RUN)[:, :, :, rs]
            nc.vector.tensor_copy(out=out, in_=in_)

        def quantise_x(b, half):
            rs = slice(half * HALF, (half + 1) * HALF)
            cols = slice(half * HALF * P, (half + 1) * HALF * P)
            nc.vector.quantize_mx(
                out=x_codes[:, b, cols].bitcast(FP8X4),
                scales=x_scales[:, b, cols],
                in_=x_grouped_of[b][:, rs].rearrange("p r q t -> p (r q t)"),
            )

        def project(out, left, left_scale, right, right_scale):
            nc.tensor.matmul_mx(
                out=out,
                lhsT=left.bitcast(FP8X4),
                lhsT_scale=left_scale,
                rhs=right.bitcast(FP8X4),
                rhs_scale=right_scale,
                start=True,
                stop=True,
            )

        def project_positions(pool, j, b, r):
            bank = pool.tile([P, COLS], F32, tag="bank")
            cols = slice(r * P, (r + 1) * P)
            project(bank[:], x_codes[:, b, cols], x_scales[:, b, cols], w_codes[:, j, :], w_scales[:, j, :])
            return bank

        units = [(j, b) for j in range(KINDS) for b in range(BATCH)]
        squares_of = {}
        sums_of = {}
        turned_of = {}
        rnorm_of = {}
        result_of = {}

        def shares(i):
            if i < len(FIRST_SHARES):
                g, t = FIRST_SHARES[i]
            else:
                g, t = LAST_SHARES if i == len(units) - 1 else SHARES
            return g, t, RUN - g - t

        def turned_groups(t):
            return [(sum(GROUPS[t][:k]), n) for k, n in enumerate(GROUPS[t])]

        def square_bank(i, place):
            j, b = units[i]
            g, t, v = shares(i)
            if place == 0:
                squares = sq_pool.tile([P, RUN, COLS], F32)
                sums = norm_pool.tile([P, RUN, HEAD_DIM], F32)
                squares_of[i] = squares
                sums_of[i] = sums
            out = squares_of[i][:, place]
            if g <= place < g + t:
                first, n = [group for group in turned_groups(t) if group[0] <= place - g][-1]
                tiles = W_TILES // n
                bank = sq_psum.tile([P, COLS], F32, tag="bank")
                cols = slice((g + first) * P, (g + first + n) * P)
                for e in range(tiles):
                    c = tiles * (place - g - first) + e
                    filters = slice(c * P, (c + 1) * P)
                    project(
                        bank[:, e * n * P : (e + 1) * n * P],
                        w_codes[:, j, filters],
                        w_scales[:, j, filters],
                        x_codes[:, b, cols],
                        x_scales[:, b, cols],
                    )
                in_ = bank[:]
            else:
                bank = project_positions(sq_psum, j, b, place)
                in_ = bank[:]
                if place >= g + t:
                    out = out.rearrange("p (d n) -> p d n", n=HEADS)
                    in_ = in_.rearrange("p (n d) -> p d n", n=HEADS)
            nc.scalar.activation(out=out, in_=in_, func=ACT.Square)

        def gpsimd_adds(i):
            g = shares(i)[0]
            squares = squares_of[i][:, 0:g].rearrange("p r (n d) -> p r n d", n=HEADS)
            for heads in (4, 2):
                nc.gpsimd.tensor_tensor(
                    out=squares[:, :, 0:heads],
                    in0=squares[:, :, 0:heads],
                    in1=squares[:, :, heads : 2 * heads],
                    op=ALU.add,
                )
            nc.gpsimd.tensor_tensor(
                out=sums_of[i][:, 0:g], in0=squares[:, :, 0], in1=squares[:, :, 1], op=ALU.add
            )

        def vector_adds(i):
            g, t, v = shares(i)
            nc.vector.tensor_reduce(
                out=sums_of[i][:, g + t : RUN],
                in_=squares_of[i][:, g + t : RUN].rearrange("p r (d n) -> p r d n", n=HEADS),
                axis=mybir.AxisListType.X,
                op=ALU.add,
            )

        def sums_banks(t):
            return [range(k, min(k + SUMS_A_BANK, t)) for k in range(0, t, SUMS_A_BANK)]

        def turn_squares(i, part):
            g, t, v = shares(i)
            positions = sums_banks(t)[part]
            if i < len(FIRST_SHARES):
                turned = mul_psum.tile([P, len(positions), P], F32, tag="bank")
            else:
                turned = turn_psum.tile([P, len(positions), P], F32, tag="turn")
            turned_of[i, part] = turned
            for first, n in turned_groups(t):
                group = squares_of[i][:, g + first : g + first + n].rearrange(
                    "p m (c q) -> p (m c) q", q=n * P
                )
                for k in range(n):
                    if first + k not in positions:
                        continue
                    for c in range(W_TILES):
                        nc.tensor.matmul(
                            turned[:, first + k - positions[0], :],
                            lhsT=group[:, c, k * P : (k + 1) * P],
                            rhs=ident_f32[:],
                            is_transpose=True,
                            start=c == 0,
                            stop=c == W_TILES - 1,
                        )

        def fold(i, part):
            g, t, v = shares(i)
            positions = sums_banks(t)[part]
            nc.vector.tensor_reduce(
                out=sums_of[i][:, g + positions[0] : g + positions[-1] + 1],
                in_=turned_of[i, part][:].rearrange("p k (h d) -> p k d h", h=2),
                axis=mybir.AxisListType.X,
                op=ALU.add,
            )

        def inverse_root(i):
            rnorm = norm_pool.tile([P, RUN, HEAD_DIM], F32)
            rnorm_of[i] = rnorm
            nc.scalar.activation(
                out=rnorm[:].rearrange("p r d -> p (r d)"),
                in_=sums_of[i][:].rearrange("p r d -> p (r d)"),
                func=ACT.Abs_reciprocal_sqrt,
                scale=1.0 / HEADS,
                bias=eps_col[:],
            )

        def multiply_bank(i, m):
            j, b = units[i]
            if m == 0:
                result = res_pool.tile([P, HEADS, RUN, HEAD_DIM], F32)
                result_of[i] = result
            side, pair = divmod(m, RUN // 2)
            heads = slice(side * HEADS // 2, (side + 1) * HEADS // 2)
            rs = slice(2 * pair, 2 * pair + 2)
            filters = slice(side * COLS // 2, (side + 1) * COLS // 2)
            bank = mul_psum.tile([P, COLS], F32, tag="bank")
            for e in range(2):
                cols = slice((2 * pair + e) * P, (2 * pair + e + 1) * P)
                project(
                    bank[:, e * COLS // 2 : (e + 1) * COLS // 2],
                    x_codes[:, b, cols],
                    x_scales[:, b, cols],
                    w_codes[:, j, filters],
                    w_scales[:, j, filters],
                )
            nc.vector.tensor_tensor(
                out=result_of[i][:, heads, rs, :].rearrange("p n r d -> p r n d"),
                in0=bank[:].rearrange("p (r n d) -> p r n d", r=2, n=HEADS // 2),
                in1=rnorm_of[i][:, rs, :].unsqueeze(2).to_broadcast([P, 2, HEADS // 2, HEAD_DIM]),
                op=ALU.mult,
            )
            if pair == RUN // 2 - 1:
                nc.sync.dma_start(
                    out=outs[j][b].rearrange("n (q r) d -> q n r d", r=RUN)[:, heads],
                    in_=result_of[i][:, heads],
                )

        filter_norm(0, 0)
        filter_norm_vector(0, 1)
        filter_norm(0, 2)
        filter_norm_vector(0, 3)
        filter_root(0)
        denominator_w(0)
        factor_w(0)
        scale_w(0)
        group_x(0, 0)
        for half in range(2):
            turn_w(0, half)
            group_w(0, half)
        quantise_x(0, 0)
        quantise_w(0, slice(0, COLS // 2))
        group_x(0, 1)
        quantise_w(0, slice(COLS // 2, COLS))

        steps = {}

        def at(slot, *step):
            steps.setdefault(slot, []).append(step)

        at(0, quantise_x, 0, 1)
        for b, (first, second, both) in enumerate(X_AT, start=1):
            at(first, group_x, b, 0)
            at(second, group_x, b, 1)
            at(both, quantise_x, b, 0)
            at(both, quantise_x, b, 1)
        for j, (norm, step, scale, turns, quantise) in enumerate(W_AT, start=1):
            for c in range(W_TILES):
                at(norm + step * c, filter_norm, j, c)
            at(norm + step * (W_TILES - 1), filter_root, j)
            at(scale - 2, denominator_w, j)
            at(scale - 1, factor_w, j)
            at(scale, scale_w, j)
            for half, slot in enumerate(turns):
                at(slot, turn_w, j, half)
                at(slot + 2, group_w, j, half)
            at(quantise, quantise_w, j, slice(0, COLS))
        for i in range(len(units)):
            g, t, v = shares(i)
            s = RUN * i
            if g:
                at(s + g - 1, gpsimd_adds, i)
            for part, positions in enumerate(sums_banks(t)):
                last = s + g + positions[-1]
                at(last + TURN_AFTER, turn_squares, i, part)
                at(last + FOLD_AFTER, fold, i, part)
            if v:
                at(s + REDUCE_AT, vector_adds, i)
            at(s + ROOT_AT, inverse_root, i)

        banks = RUN * len(units)
        for slot in range(banks + LAG):
            if slot < banks:
                square_bank(slot // RUN, slot % RUN)
            for action, *arguments in steps.get(slot, ()):
                action(*arguments)
            if slot >= LAG:
                multiply_bank((slot - LAG) // RUN, (slot - LAG) % RUN)
